import numpy as np
import ml_dtypes


def mxq(x, axis, fmt="e4m3"):
    dtype, down = {"e4m3": (ml_dtypes.float8_e4m3fn, 7), "e5m2": (ml_dtypes.float8_e5m2, 14)}[fmt]
    v = np.moveaxis(np.asarray(x, np.float32).astype(ml_dtypes.bfloat16).astype(np.float64), axis, -1)
    blocks = v.reshape(v.shape[:-1] + (-1, 32))
    amax = np.abs(blocks).max(-1, keepdims=True)
    byte = np.maximum(np.where(amax > 0, np.frexp(amax)[1] - 1 + 127, 0) - down, 1)
    scale = np.exp2(byte - 127.0)
    codes = (blocks / scale).astype(np.float32).astype(dtype).astype(np.float64)
    return np.moveaxis((codes * scale).reshape(v.shape), -1, axis)


WIDE = False


def mx_kscale(k):
    if not WIDE:
        return np.ones(k)
    levels = np.array([10, -10, 5, -5, 0])
    a = np.random.permutation(np.resize(levels, k // 512 * 4)).reshape(k // 512, 4)
    idx = np.arange(k)
    return np.exp2(a[idx // 512, idx % 128 // 32])


BF16 = ml_dtypes.bfloat16


def bf(x):
    return np.asarray(x, np.float32).astype(BF16)


def f64(x):
    return np.asarray(x).astype(np.float64)


E2M1 = np.array([0.0, 0.5, 1.0, 1.5, 2.0, 3.0, 4.0, 6.0, -0.0, -0.5, -1.0, -1.5, -2.0, -3.0, -4.0, -6.0])


def pack_weight(w, fmt):
    k, n = w.shape
    w = f64(bf(w)).reshape(k // 32, 32, n)
    amax = np.abs(w).max(1)
    if fmt == "e4m3":
        byte = np.frexp(amax)[1] - 1 + 127 - 7
    else:
        mant, ex = np.frexp(amax / 6.0)
        byte = np.where(mant > 0.5, ex, ex - 1) + 127
    byte = np.clip(np.where(amax > 0, byte, 1), 1, 254)
    scaled = (w * np.exp2(127.0 - byte)[:, None, :]).reshape(k, n).astype(np.float32)
    by_word = np.ascontiguousarray(scaled.reshape(k // 512, 128, 4, n).transpose(0, 1, 3, 2))
    if fmt == "e4m3":
        words = by_word.astype(ml_dtypes.float8_e4m3fn).view(np.uint8)
    else:
        c = by_word.astype(ml_dtypes.float4_e2m1fn).view(np.uint8) & 0xF
        words = c[..., 0::2] | (c[..., 1::2] << 4)
    return np.ascontiguousarray(words), np.ascontiguousarray(byte.astype(np.uint8).reshape(k // 512, 16, n))


def unpack_weight(words, scales, fmt):
    g, p, n, _ = words.shape
    if fmt == "e4m3":
        vals = np.ascontiguousarray(words).view(ml_dtypes.float8_e4m3fn).astype(np.float64)
    else:
        nib = np.empty((g, p, n, 4), np.uint8)
        nib[..., 0::2] = words & 0xF
        nib[..., 1::2] = words >> 4
        vals = E2M1[nib]
    vals = vals * np.repeat(np.exp2(scales.astype(np.float64) - 127.0), 8, axis=1)[..., None]
    return vals.transpose(0, 1, 3, 2).reshape(g * 512, n)


N, C_IN, H_IN, W_IN, C_OUT, K, PAD, STRIDE = 128, 64, 9, 9, 128, 4, 1, 1
H_OUT = (H_IN - K + 2 * PAD) // STRIDE + 1
W_OUT = (W_IN - K + 2 * PAD) // STRIDE + 1
RF = C_IN * K * K
NUM_PIX = H_OUT * W_OUT


def _unfold(x):
    n = x.shape[0]
    xp = np.pad(x, ((0, 0), (0, 0), (PAD, PAD), (PAD, PAD)))
    patches = []
    for i in range(K):
        for j in range(K):
            patches.append(xp[:, :, i:i + H_OUT * STRIDE:STRIDE, j:j + W_OUT * STRIDE:STRIDE])
    p = np.stack(patches, axis=2)
    return p.reshape(n, RF, NUM_PIX)


def setup_inputs():
    sc = mx_kscale(RF)[::K * K]
    s = np.repeat(sc, K * K)
    x = bf(np.random.standard_normal((N, C_IN, H_IN, W_IN)) * sc[None, :, None, None])
    stack = np.random.standard_normal((C_OUT, RF, NUM_PIX)) / np.sqrt(RF) / s[None, :, None]
    words, scales = pack_weight(stack.reshape(-1, NUM_PIX), "e4m3")
    bias = bf(np.random.standard_normal((C_OUT, NUM_PIX)) * 0.3)
    return {"x": x, "filters_words": words, "filters_scales": scales, "bias": bias}


def reference(x, filters_words, filters_scales, bias):
    x = f64(x)
    f_hat = _unfold(x)
    fq = mxq(f_hat, 1, "e4m3")
    wq = unpack_weight(filters_words, filters_scales, "e4m3").reshape(C_OUT, RF, NUM_PIX)
    g = (fq.transpose(2, 0, 1) @ wq.transpose(2, 1, 0)).transpose(1, 2, 0)
    g = g + f64(bias)
    return g.reshape(x.shape[0], C_OUT, H_OUT, W_OUT)

@@ -1,0 +1,312 @@
+from contextlib import ExitStack
+
+import concourse.mybir as mybir
+from concourse.masks import make_identity
+
+BF16 = mybir.dt.bfloat16
+F32 = mybir.dt.float32
+I32 = mybir.dt.int32
+U32 = mybir.dt.uint32
+U8 = mybir.dt.uint8
+FP8X4 = mybir.dt.float8_e4m3fn_x4
+
+P = 128
+IMAGES = 128
+C_IN = 64
+SIDE_IN = 9
+SIDE_OUT = 8
+TAPS = 4
+C_OUT = 128
+PIXELS = SIDE_OUT * SIDE_OUT
+PASSES = 2
+ROW = SIDE_IN + 1
+ROW_WORDS = ROW // 2
+BANK_PLANES = 4
+ROW_BANKS = 3
+O_CHUNK = 32
+CHUNKS = C_OUT // O_CHUNK
+CHUNK_GROUPS = PASSES * O_CHUNK
+PX_GROUP = 4
+GROUPS_ROW = SIDE_OUT // PX_GROUP
+N_MOVING = O_CHUNK * PX_GROUP
+BANK = 512
+LAG = 2
+CATCH_UP = 2
+ROW_TILES = PASSES * TAPS // 2
+X_STEPS = SIDE_OUT - 4
+
+X_HALVES = (slice(0, C_IN // PASSES), slice(C_IN // PASSES, C_IN))
+
+FLOPS = 2 * IMAGES * C_IN * TAPS * TAPS * C_OUT * PIXELS
+
+
+def tile_localconv2dlayer_e_kernel(tc, x, filters_words, filters_scales, bias, out):
+    nc = tc.nc
+    with ExitStack() as stack:
+        keep = stack.enter_context(tc.tile_pool(name="keep", bufs=1))
+        raw_pool = stack.enter_context(tc.tile_pool(name="raw_filters", bufs=CHUNKS))
+        moving_pool = stack.enter_context(tc.tile_pool(name="moving", bufs=2))
+        bias_pool = stack.enter_context(tc.tile_pool(name="bias", bufs=3))
+        out_pool = stack.enter_context(tc.tile_pool(name="result", bufs=3))
+        grouped_pool = stack.enter_context(tc.tile_pool(name="grouped", bufs=3))
+        bank_pool = stack.enter_context(tc.psum_pool(name="transposed", bufs=4))
+        acc_pool = stack.enter_context(tc.psum_pool(name="sums", bufs=2))
+
+        identity = keep.tile([P, P], F32, name="identity")
+        zeros = keep.tile([P, 2 * P], BF16, name="zeros")
+        rows = [keep.tile([P, IMAGES, 2 * ROW_BANKS * BANK_PLANES], BF16, name="row%d" % b) for b in range(2)]
+        padded = [keep.tile([P, C_IN, TAPS, ROW], BF16, name="padded%d" % b) for b in range(2)]
+        codes = keep.tile([P, SIDE_OUT, PASSES, SIDE_OUT * IMAGES], U32, name="codes", align_bytes=64)
+        code_scales = keep.tile([P, SIDE_OUT, TAPS * IMAGES], U8, name="code_scales", align_bytes=64)
+        filter_scales = keep.tile(
+            [P, CHUNKS, SIDE_OUT * GROUPS_ROW, PASSES, N_MOVING], U8, name="filter_scales", align_bytes=64
+        )
+
+        raws = {}
+
+        def raw_scales(chunk, partitions):
+            return (
+                codes[partitions, SIDE_OUT - 2 + chunk // PASSES, chunk % PASSES, :]
+                .bitcast(I32)
+                .rearrange("p (g w) -> p g w", w=PIXELS // 4)
+            )
+
+        def load_filters(chunk):
+            groups = slice(CHUNK_GROUPS * chunk, CHUNK_GROUPS * (chunk + 1))
+            for quadrant in range(4):
+                nc.sync.dma_start(
+                    out=raw_scales(chunk, slice(32 * quadrant, 32 * quadrant + 4)),
+                    in_=filters_scales[groups, 4 * quadrant : 4 * quadrant + 4, :]
+                    .rearrange("g r n -> r g n")
+                    .bitcast(I32),
+                )
+            raw = raw_pool.tile([P, CHUNK_GROUPS, PIXELS], I32, name="raw")
+            nc.sync.dma_start(
+                out=raw[:], in_=filters_words[groups].rearrange("g p n t -> p g (n t)").bitcast(I32)
+            )
+            raws[chunk] = raw
+
+        def spread_scales(chunk):
+            nc.vector.tensor_copy(
+                out=filter_scales[:, chunk].bitcast(I32),
+                in_=raw_scales(chunk, slice(0, P)).rearrange("p (o f) g -> p g f o", f=PASSES),
+            )
+
+        def fill_tile(h, i):
+            f, e = divmod(i, TAPS // 2)
+            values = rows[h % 2]
+            first = ROW * f + 2 * e
+            grouped = grouped_pool.tile([P, 2, 2, IMAGES, TAPS], BF16, name="grouped", align_bytes=64)
+            nc.scalar.copy(
+                out=grouped[:].bitcast(F32)[:, 0, :, :, :],
+                in_=values[:].bitcast(F32)[:, :, first // 2 : first // 2 + TAPS].rearrange("p n (b u) -> p b n u", u=2),
+            )
+            odd_copy = nc.scalar.copy if i == ROW_TILES - 1 else nc.vector.tensor_copy
+            odd_copy(
+                out=grouped[:, 1, :, :, :],
+                in_=values[:, :, first + 1 : first + 1 + 2 * TAPS].rearrange("p n (b j) -> p b n j", j=TAPS),
+            )
+            return (f, e, grouped)
+
+        def quantise(h, item):
+            f, e, grouped = item
+            columns = slice(TAPS * IMAGES * e, TAPS * IMAGES * (e + 1))
+            nc.vector.quantize_mx(
+                out=codes[:, h, f, columns].bitcast(FP8X4),
+                scales=code_scales[4 * (2 * f + e) : P, h, :],
+                in_=grouped[:].rearrange("p s b n j -> p (s b n j)"),
+            )
+
+        biases = {}
+        results = {}
+        first_step = [LAG * chunk for chunk in range(CHUNKS)]
+        first_step[CHUNKS - 1] -= 1
+        steps = []
+        done = [0] * CHUNKS
+        for step_no in range(first_step[CHUNKS - 1] + SIDE_OUT // CATCH_UP):
+            jobs = []
+            for chunk in range(CHUNKS):
+                if step_no >= first_step[chunk]:
+                    upto = min(done[chunk] + CATCH_UP, step_no + 1, SIDE_OUT)
+                    jobs.extend((chunk, h) for h in range(done[chunk], upto))
+                    done[chunk] = upto
+            steps.append(jobs)
+        units = [unit for jobs in steps for unit in jobs]
+        movings = {}
+        sums_of = {}
+
+        def open_chunk(chunk, bias_from, result_from):
+            bias_sb = bias_from.tile([P, O_CHUNK, PIXELS], BF16, name="bias_sb")
+            nc.sync.dma_start(
+                out=bias_sb[:].rearrange("p o n -> p (o n)"),
+                in_=bias[O_CHUNK * chunk : O_CHUNK * (chunk + 1), :].rearrange("o n -> (o n)").partition_broadcast(P),
+            )
+            biases[chunk] = bias_sb
+            result = result_from.tile([P, O_CHUNK, PIXELS], F32, name="result")
+            results[chunk] = result
+
+        def regroup_filters(k):
+            chunk, h = units[k]
+            moving = moving_pool.tile([P, GROUPS_ROW, PASSES, N_MOVING], I32, name="moving", align_bytes=64)
+            nc.vector.tensor_copy(
+                out=moving[:].rearrange("p g f (o q) -> p g f o q", q=PX_GROUP),
+                in_=raws[chunk][:]
+                .rearrange("p (o f) n -> p o f n", f=PASSES)[:, :, :, SIDE_OUT * h : SIDE_OUT * (h + 1)]
+                .rearrange("p o f (g q) -> p g f o q", q=PX_GROUP),
+            )
+            movings[k] = moving
+
+        def multiply(k):
+            chunk, h = units[k]
+            moving = movings[k]
+            sums = acc_pool.tile([P, GROUPS_ROW * BANK], F32, name="sums")
+            for g in range(GROUPS_ROW):
+                for q in range(PX_GROUP):
+                    block = IMAGES * (2 * q + g)
+                    in_call = IMAGES * (2 * (q % 2) + g)
+                    for f in range(PASSES):
+                        nc.tensor.matmul_mx(
+                            out=sums[:, BANK * g + N_MOVING * q : BANK * g + N_MOVING * (q + 1)],
+                            lhsT=codes[:, h, f, block : block + IMAGES].bitcast(FP8X4),
+                            lhsT_scale=code_scales[4 * (2 * f + q // 2) : P, h, in_call : in_call + IMAGES],
+                            rhs=moving[:, g, f, :].bitcast(FP8X4),
+                            rhs_scale=filter_scales[:, chunk, GROUPS_ROW * h + g, f, :],
+                            start=(f == 0),
+                            stop=(f == PASSES - 1),
+                        )
+            sums_of[k] = sums
+
+        def add_bias(k):
+            chunk, h = units[k]
+            sums = sums_of[k]
+            step = N_MOVING + 1
+            for g in range(GROUPS_ROW):
+                if g == 0:
+                    own = sums[:, 0 : PX_GROUP * step].rearrange("p (q r) -> p q r", r=step)[
+                        :, :, 0 : N_MOVING - 3 : PX_GROUP
+                    ]
+                else:
+                    own = sums[:, 2 * BANK - PX_GROUP * step : 2 * BANK].rearrange("p (q r) -> p q r", r=step)[
+                        :, :, PX_GROUP:step:PX_GROUP
+                    ]
+                pixels = slice(SIDE_OUT * h + PX_GROUP * g, SIDE_OUT * h + PX_GROUP * (g + 1))
+                nc.vector.tensor_tensor(
+                    out=results[chunk][:, :, pixels],
+                    in0=own.rearrange("p q o -> p o q"),
+                    in1=biases[chunk][:, :, pixels],
+                    op=mybir.AluOpType.add,
+                )
+            if h == SIDE_OUT - 1:
+                nc.scalar.dma_start(
+                    out=out[:, O_CHUNK * chunk : O_CHUNK * (chunk + 1), :, :].rearrange("n o h w -> n o (h w)"),
+                    in_=results[chunk][:],
+                )
+
+        def copy_out(h, banks):
+            words = rows[h % 2][:].bitcast(F32)
+            for bank in range(ROW_BANKS):
+                nc.scalar.copy(
+                    out=words[:, :, BANK_PLANES * bank : BANK_PLANES * (bank + 1)],
+                    in_=banks[bank][:].rearrange("p a n -> p n a"),
+                )
+
+        def run_step(step_no, transpose_row, pad_row):
+            jobs = steps[step_no] if step_no >= 0 else []
+            first_unit = sum(len(earlier) for earlier in steps[: max(step_no, 0)])
+            row = step_no + 1
+            previous = None
+            banks = None
+            for i in range(max(ROW_TILES, len(jobs))):
+                if row < SIDE_OUT and i < ROW_TILES:
+                    filled = fill_tile(row, i)
+                    if previous is not None:
+                        quantise(row, previous)
+                    previous = filled
+                if i < len(jobs):
+                    k = first_unit + i
+                    multiply(k)
+                    if k + 1 < len(units):
+                        regroup_filters(k + 1)
+                    if k >= 1:
+                        add_bias(k - 1)
+                if i == 0 and row + 1 < SIDE_OUT:
+                    banks = transpose_row(row + 1)
+            if previous is not None:
+                quantise(row, previous)
+            if banks is not None:
+                copy_out(row + 1, banks)
+            if row + 2 < SIDE_OUT:
+                pad_row(row + 2)
+            for chunk in range(1, CHUNKS):
+                if first_step[chunk] == row:
+                    spread_scales(chunk)
+
+        stack.enter_context(tc.manual_schedule())
+        with tc.tile_pool(name="early", bufs=1) as early:
+            x_sb = early.tile([P, C_IN, SIDE_IN * SIDE_IN], BF16, name="x_sb")
+
+            def pad_row(h):
+                tile = padded[h % 2]
+                if h == 0:
+                    for channels in X_HALVES:
+                        nc.vector.tensor_copy(
+                            out=tile[:, channels, 1:TAPS, 1:ROW],
+                            in_=x_sb[:, channels, 0 : SIDE_IN * (TAPS - 1)].rearrange("p c (i w) -> p c i w", w=SIDE_IN),
+                        )
+                    return
+                nc.scalar.copy(
+                    out=tile[:].bitcast(F32)[:, :, 0 : TAPS - 1, :],
+                    in_=padded[(h - 1) % 2][:].bitcast(F32)[:, :, 1:TAPS, :],
+                )
+                bottom = h + TAPS - 2
+                if bottom < SIDE_IN:
+                    nc.scalar.copy(
+                        out=tile[:, :, TAPS - 1, 1:ROW], in_=x_sb[:, :, SIDE_IN * bottom : SIDE_IN * (bottom + 1)]
+                    )
+                else:
+                    nc.scalar.copy(
+                        out=tile[:, :, TAPS - 1, 1:ROW],
+                        in_=zeros[:, 0:SIDE_IN].unsqueeze(1).to_broadcast([P, C_IN, SIDE_IN]),
+                    )
+
+            def transpose_row(h):
+                source = padded[h % 2][:].bitcast(F32).rearrange("p c i a -> p (c i) a")
+                banks = []
+                for bank in range(ROW_BANKS):
+                    planes = bank_pool.tile([P, BANK_PLANES, IMAGES], F32, name="planes")
+                    for m in range(BANK_PLANES):
+                        f, a = divmod(BANK_PLANES * bank + m, ROW_WORDS)
+                        if f < PASSES:
+                            nc.tensor.transpose(planes[:, m, :], source[:, P * f : P * (f + 1), a], identity[:])
+                        else:
+                            nc.tensor.transpose(planes[:, m, :], zeros[:].bitcast(F32), identity[:])
+                    banks.append(planes)
+                return banks
+
+            for channels in X_HALVES:
+                nc.sync.dma_start(out=x_sb[:, channels, :], in_=x[:, channels, :, :].rearrange("n c h w -> n c (h w)"))
+            for chunk in range(CHUNKS):
+                nc.gpsimd.memset(codes[:, SIDE_OUT - 2 + chunk // PASSES, chunk % PASSES, :].bitcast(F32), 0.0)
+            for b in range(2):
+                nc.vector.memset(padded[b][:].bitcast(I32), 0)
+            nc.vector.memset(zeros[:].bitcast(I32), 0)
+            make_identity(nc, identity[:])
+            for chunk in range(CHUNKS):
+                load_filters(chunk)
+                if chunk < CHUNKS - 1:
+                    open_chunk(chunk, bias_pool, out_pool)
+
+            pad_row(0)
+            pad_row(1)
+            copy_out(0, transpose_row(0))
+            spread_scales(0)
+            run_step(-1, transpose_row, pad_row)
+            regroup_filters(0)
+            for step_no in range(X_STEPS):
+                run_step(step_no, transpose_row, pad_row)
+
+        with tc.tile_pool(name="late", bufs=1, reuse_waits="tile") as late:
+            open_chunk(CHUNKS - 1, late, late)
+            for step_no in range(X_STEPS, len(steps)):
+                run_step(step_no, transpose_row, pad_row)
+            add_bias(len(units) - 1)

@@ -21,6 +21,7 @@ PIXELS = SIDE_OUT * SIDE_OUT
 PASSES = 2
 ROW = SIDE_IN + 1
 ROW_WORDS = ROW // 2
+ROLL = 8
 BANK_PLANES = 4
 ROW_BANKS = 3
 O_CHUNK = 32
@@ -30,10 +31,11 @@ PX_GROUP = 4
 GROUPS_ROW = SIDE_OUT // PX_GROUP
 N_MOVING = O_CHUNK * PX_GROUP
 BANK = 512
-LAG = 2
-CATCH_UP = 2
+FIRST_TICK = (5, 16, 20, 28)
 ROW_TILES = PASSES * TAPS // 2
-X_STEPS = SIDE_OUT - 4
+ROWS_V = 4
+TICKS = SIDE_OUT * ROW_TILES
+X_TICKS = ROW_TILES * (SIDE_OUT - 3)
 
 X_HALVES = (slice(0, C_IN // PASSES), slice(C_IN // PASSES, C_IN))
 
@@ -55,7 +57,7 @@ def tile_localconv2dlayer_e_kernel(tc, x, filters_words, filters_scales, bias, o
         identity = keep.tile([P, P], F32, name="identity")
         zeros = keep.tile([P, 2 * P], BF16, name="zeros")
         rows = [keep.tile([P, IMAGES, 2 * ROW_BANKS * BANK_PLANES], BF16, name="row%d" % b) for b in range(2)]
-        padded = [keep.tile([P, C_IN, TAPS, ROW], BF16, name="padded%d" % b) for b in range(2)]
+        padded = keep.tile([P, TAPS * C_IN + ROLL, ROW], BF16, name="padded")
         codes = keep.tile([P, SIDE_OUT, PASSES, SIDE_OUT * IMAGES], U32, name="codes", align_bytes=64)
         code_scales = keep.tile([P, SIDE_OUT, TAPS * IMAGES], U8, name="code_scales", align_bytes=64)
         filter_scales = keep.tile(
@@ -101,7 +103,7 @@ def tile_localconv2dlayer_e_kernel(tc, x, filters_words, filters_scales, bias, o
                 out=grouped[:].bitcast(F32)[:, 0, :, :, :],
                 in_=values[:].bitcast(F32)[:, :, first // 2 : first // 2 + TAPS].rearrange("p n (b u) -> p b n u", u=2),
             )
-            odd_copy = nc.scalar.copy if i == ROW_TILES - 1 else nc.vector.tensor_copy
+            odd_copy = nc.scalar.copy if h >= ROWS_V and i >= ROW_TILES // 2 else nc.vector.tensor_copy
             odd_copy(
                 out=grouped[:, 1, :, :, :],
                 in_=values[:, :, first + 1 : first + 1 + 2 * TAPS].rearrange("p n (b j) -> p b n j", j=TAPS),
@@ -119,19 +121,19 @@ def tile_localconv2dlayer_e_kernel(tc, x, filters_words, filters_scales, bias, o
 
         biases = {}
         results = {}
-        first_step = [LAG * chunk for chunk in range(CHUNKS)]
-        first_step[CHUNKS - 1] -= 1
-        steps = []
+        plan = []
         done = [0] * CHUNKS
-        for step_no in range(first_step[CHUNKS - 1] + SIDE_OUT // CATCH_UP):
-            jobs = []
-            for chunk in range(CHUNKS):
-                if step_no >= first_step[chunk]:
-                    upto = min(done[chunk] + CATCH_UP, step_no + 1, SIDE_OUT)
-                    jobs.extend((chunk, h) for h in range(done[chunk], upto))
-                    done[chunk] = upto
-            steps.append(jobs)
-        units = [unit for jobs in steps for unit in jobs]
+        while sum(done) < CHUNKS * SIDE_OUT:
+            tick = len(plan)
+            ready = [
+                chunk
+                for chunk in range(CHUNKS)
+                if tick >= FIRST_TICK[chunk] and done[chunk] < min(tick // ROW_TILES - (tick % ROW_TILES == 0), SIDE_OUT)
+            ]
+            plan.append((ready[0], done[ready[0]]) if ready else None)
+            if ready:
+                done[ready[0]] += 1
+        units = [unit for unit in plan if unit is not None]
         movings = {}
         sums_of = {}
 
@@ -210,74 +212,72 @@ def tile_localconv2dlayer_e_kernel(tc, x, filters_words, filters_scales, bias, o
                     in_=banks[bank][:].rearrange("p a n -> p n a"),
                 )
 
-        def run_step(step_no, transpose_row, pad_row):
-            jobs = steps[step_no] if step_no >= 0 else []
-            first_unit = sum(len(earlier) for earlier in steps[: max(step_no, 0)])
-            row = step_no + 1
-            previous = None
-            banks = None
-            for i in range(max(ROW_TILES, len(jobs))):
-                if row < SIDE_OUT and i < ROW_TILES:
-                    filled = fill_tile(row, i)
-                    if previous is not None:
-                        quantise(row, previous)
-                    previous = filled
-                if i < len(jobs):
-                    k = first_unit + i
-                    multiply(k)
-                    if k + 1 < len(units):
-                        regroup_filters(k + 1)
-                    if k >= 1:
-                        add_bias(k - 1)
-                if i == 0 and row + 1 < SIDE_OUT:
-                    banks = transpose_row(row + 1)
-            if previous is not None:
-                quantise(row, previous)
-            if banks is not None:
-                copy_out(row + 1, banks)
-            if row + 2 < SIDE_OUT:
-                pad_row(row + 2)
-            for chunk in range(1, CHUNKS):
-                if first_step[chunk] == row:
-                    spread_scales(chunk)
+        filled = {}
+        issued = {"units": 0, "regroups": 0}
 
+        def regroup_next():
+            k = issued["regroups"]
+            regroup_filters(k)
+            issued["regroups"] = k + 1
+
+        def run_tick(tick, transpose_row, pad_row):
+            if tick < TICKS:
+                filled[tick] = fill_tile(tick // ROW_TILES, tick % ROW_TILES)
+            if tick - 1 in filled:
+                quantise((tick - 1) // ROW_TILES, filled[tick - 1])
+            if tick < len(plan) and plan[tick] is not None:
+                k = issued["units"]
+                if issued["regroups"] == k:
+                    regroup_next()
+                multiply(k)
+                if tick + 1 < len(plan) and plan[tick + 1] is not None:
+                    ahead = plan[tick + 1]
+                    if tick + 1 != FIRST_TICK[ahead[0]]:
+                        regroup_next()
+                if k >= 1:
+                    add_bias(k - 1)
+                issued["units"] = k + 1
+            for chunk in range(CHUNKS):
+                if tick + 1 == FIRST_TICK[chunk]:
+                    spread_scales(chunk)
+            row, i = divmod(tick, ROW_TILES)
+            if i == 2 and row + 1 < SIDE_OUT:
+                copy_out(row + 1, banks_of[row + 1])
+            if i == 3 and row + 2 < SIDE_OUT:
+                pad_row(row + 2)
+                banks_of[row + 2] = transpose_row(row + 2)
+
+        banks_of = {}
         stack.enter_context(tc.manual_schedule())
         with tc.tile_pool(name="early", bufs=1) as early:
             x_sb = early.tile([P, C_IN, SIDE_IN * SIDE_IN], BF16, name="x_sb")
 
             def pad_row(h):
-                tile = padded[h % 2]
                 if h == 0:
                     for channels in X_HALVES:
                         nc.vector.tensor_copy(
-                            out=tile[:, channels, 1:TAPS, 1:ROW],
+                            out=padded[:, TAPS * channels.start : TAPS * channels.stop, :].rearrange(
+                                "p (c i) w -> p c i w", i=TAPS
+                            )[:, :, 1:TAPS, 1:ROW],
                             in_=x_sb[:, channels, 0 : SIDE_IN * (TAPS - 1)].rearrange("p c (i w) -> p c i w", w=SIDE_IN),
                         )
                     return
-                nc.scalar.copy(
-                    out=tile[:].bitcast(F32)[:, :, 0 : TAPS - 1, :],
-                    in_=padded[(h - 1) % 2][:].bitcast(F32)[:, :, 1:TAPS, :],
-                )
                 bottom = h + TAPS - 2
+                place = padded[:, bottom + 1 : bottom + 1 + TAPS * (C_IN - 1) + 1 : TAPS, 1:ROW]
                 if bottom < SIDE_IN:
-                    nc.scalar.copy(
-                        out=tile[:, :, TAPS - 1, 1:ROW], in_=x_sb[:, :, SIDE_IN * bottom : SIDE_IN * (bottom + 1)]
-                    )
+                    nc.scalar.copy(out=place, in_=x_sb[:, :, SIDE_IN * bottom : SIDE_IN * (bottom + 1)])
                 else:
-                    nc.scalar.copy(
-                        out=tile[:, :, TAPS - 1, 1:ROW],
-                        in_=zeros[:, 0:SIDE_IN].unsqueeze(1).to_broadcast([P, C_IN, SIDE_IN]),
-                    )
+                    nc.scalar.copy(out=place, in_=zeros[:, 0:SIDE_IN].unsqueeze(1).to_broadcast([P, C_IN, SIDE_IN]))
 
             def transpose_row(h):
-                source = padded[h % 2][:].bitcast(F32).rearrange("p c i a -> p (c i) a")
+                source = padded[:].bitcast(F32)
                 banks = []
                 for bank in range(ROW_BANKS):
                     planes = bank_pool.tile([P, BANK_PLANES, IMAGES], F32, name="planes")
                     for m in range(BANK_PLANES):
                         f, a = divmod(BANK_PLANES * bank + m, ROW_WORDS)
                         if f < PASSES:
-                            nc.tensor.transpose(planes[:, m, :], source[:, P * f : P * (f + 1), a], identity[:])
+                            nc.tensor.transpose(planes[:, m, :], source[:, h + P * f : h + P * (f + 1), a], identity[:])
                         else:
                             nc.tensor.transpose(planes[:, m, :], zeros[:].bitcast(F32), identity[:])
                     banks.append(planes)
@@ -287,8 +287,7 @@ def tile_localconv2dlayer_e_kernel(tc, x, filters_words, filters_scales, bias, o
                 nc.sync.dma_start(out=x_sb[:, channels, :], in_=x[:, channels, :, :].rearrange("n c h w -> n c (h w)"))
             for chunk in range(CHUNKS):
                 nc.gpsimd.memset(codes[:, SIDE_OUT - 2 + chunk // PASSES, chunk % PASSES, :].bitcast(F32), 0.0)
-            for b in range(2):
-                nc.vector.memset(padded[b][:].bitcast(I32), 0)
+            nc.vector.memset(padded[:].bitcast(I32), 0)
             nc.vector.memset(zeros[:].bitcast(I32), 0)
             make_identity(nc, identity[:])
             for chunk in range(CHUNKS):
@@ -297,16 +296,14 @@ def tile_localconv2dlayer_e_kernel(tc, x, filters_words, filters_scales, bias, o
                     open_chunk(chunk, bias_pool, out_pool)
 
             pad_row(0)
-            pad_row(1)
             copy_out(0, transpose_row(0))
-            spread_scales(0)
-            run_step(-1, transpose_row, pad_row)
-            regroup_filters(0)
-            for step_no in range(X_STEPS):
-                run_step(step_no, transpose_row, pad_row)
+            pad_row(1)
+            banks_of[1] = transpose_row(1)
+            for tick in range(X_TICKS):
+                run_tick(tick, transpose_row, pad_row)
 
         with tc.tile_pool(name="late", bufs=1, reuse_waits="tile") as late:
             open_chunk(CHUNKS - 1, late, late)
-            for step_no in range(X_STEPS, len(steps)):
-                run_step(step_no, transpose_row, pad_row)
+            for tick in range(X_TICKS, len(plan)):
+                run_tick(tick, transpose_row, pad_row)
             add_bias(len(units) - 1)

@@ -24,18 +24,22 @@ ROW_WORDS = ROW // 2
 ROLL = 8
 BANK_PLANES = 4
 ROW_BANKS = 3
-O_CHUNK = 32
-CHUNKS = C_OUT // O_CHUNK
-CHUNK_GROUPS = PASSES * O_CHUNK
-PX_GROUP = 4
-GROUPS_ROW = SIDE_OUT // PX_GROUP
-N_MOVING = O_CHUNK * PX_GROUP
+HALVES = 2
+O_HALF = C_OUT // HALVES
+HALF_GROUPS = PASSES * O_HALF
+SCALE_ROWS = 16
+PAIR = 2
+ROW_PAIRS = SIDE_OUT // PAIR
+N_MOVING = PAIR * O_HALF
 BANK = 512
-FIRST_TICK = (5, 16, 20, 28)
+BANK_PX = 4
+ROW_SUM_BANKS = SIDE_OUT // BANK_PX
 ROW_TILES = PASSES * TAPS // 2
 ROWS_V = 4
 TICKS = SIDE_OUT * ROW_TILES
 X_TICKS = ROW_TILES * (SIDE_OUT - 3)
+SCALE_TICK = 2
+FIRST_TICK = (16, 24)
 
 X_HALVES = (slice(0, C_IN // PASSES), slice(C_IN // PASSES, C_IN))
 
@@ -46,10 +50,8 @@ def tile_localconv2dlayer_e_kernel(tc, x, filters_words, filters_scales, bias, o
     nc = tc.nc
     with ExitStack() as stack:
         keep = stack.enter_context(tc.tile_pool(name="keep", bufs=1))
-        raw_pool = stack.enter_context(tc.tile_pool(name="raw_filters", bufs=CHUNKS))
+        raw_pool = stack.enter_context(tc.tile_pool(name="raw_filters", bufs=HALVES))
         moving_pool = stack.enter_context(tc.tile_pool(name="moving", bufs=2))
-        bias_pool = stack.enter_context(tc.tile_pool(name="bias", bufs=3))
-        out_pool = stack.enter_context(tc.tile_pool(name="result", bufs=3))
         grouped_pool = stack.enter_context(tc.tile_pool(name="grouped", bufs=3))
         bank_pool = stack.enter_context(tc.psum_pool(name="transposed", bufs=4))
         acc_pool = stack.enter_context(tc.psum_pool(name="sums", bufs=2))
@@ -60,38 +62,46 @@ def tile_localconv2dlayer_e_kernel(tc, x, filters_words, filters_scales, bias, o
         padded = keep.tile([P, TAPS * C_IN + ROLL, ROW], BF16, name="padded")
         codes = keep.tile([P, SIDE_OUT, PASSES, SIDE_OUT * IMAGES], U32, name="codes", align_bytes=64)
         code_scales = keep.tile([P, SIDE_OUT, TAPS * IMAGES], U8, name="code_scales", align_bytes=64)
-        filter_scales = keep.tile(
-            [P, CHUNKS, SIDE_OUT * GROUPS_ROW, PASSES, N_MOVING], U8, name="filter_scales", align_bytes=64
-        )
+        filter_scales = keep.tile([P, HALVES, PASSES, PIXELS * O_HALF], U8, name="filter_scales", align_bytes=64)
 
-        raws = {}
+        scale_sets = HALVES * PASSES * SCALE_ROWS
+        scales_loaded = codes[:, SIDE_OUT - 1, 0, :]
+        scales_by_pixel = codes[:, SIDE_OUT - 1, 1, :]
 
-        def raw_scales(chunk, partitions):
-            return (
-                codes[partitions, SIDE_OUT - 2 + chunk // PASSES, chunk % PASSES, :]
-                .bitcast(I32)
-                .rearrange("p (g w) -> p g w", w=PIXELS // 4)
-            )
-
-        def load_filters(chunk):
-            groups = slice(CHUNK_GROUPS * chunk, CHUNK_GROUPS * (chunk + 1))
-            for quadrant in range(4):
-                nc.sync.dma_start(
-                    out=raw_scales(chunk, slice(32 * quadrant, 32 * quadrant + 4)),
-                    in_=filters_scales[groups, 4 * quadrant : 4 * quadrant + 4, :]
-                    .rearrange("g r n -> r g n")
-                    .bitcast(I32),
-                )
-            raw = raw_pool.tile([P, CHUNK_GROUPS, PIXELS], I32, name="raw")
+        def load_scales(half):
+            sets = slice(PASSES * SCALE_ROWS * half, PASSES * SCALE_ROWS * (half + 1))
             nc.sync.dma_start(
-                out=raw[:], in_=filters_words[groups].rearrange("g p n t -> p g (n t)").bitcast(I32)
+                out=scales_loaded[sets, :].bitcast(I32).rearrange("z (o w) -> z o w", o=O_HALF),
+                in_=filters_scales[HALF_GROUPS * half : HALF_GROUPS * (half + 1)]
+                .rearrange("g r n -> (g r) n")
+                .rearrange("(o z) n -> z o n", z=PASSES * SCALE_ROWS)
+                .bitcast(I32),
             )
-            raws[chunk] = raw
 
-        def spread_scales(chunk):
+        def reorder_scales():
             nc.vector.tensor_copy(
-                out=filter_scales[:, chunk].bitcast(I32),
-                in_=raw_scales(chunk, slice(0, P)).rearrange("p (o f) g -> p g f o", f=PASSES),
+                out=scales_by_pixel[:].bitcast(U8).rearrange("z (n o) -> z n o", o=O_HALF),
+                in_=scales_loaded[:].bitcast(U8).rearrange("z (o n) -> z n o", o=O_HALF),
+            )
+
+        def move_scales(half, f, quadrants=(0, 1, 2, 3)):
+            for quadrant in quadrants:
+                source = SCALE_ROWS * (PASSES * half + f) + 4 * quadrant
+                nc.sync.dma_start(
+                    out=filter_scales[32 * quadrant : 32 * quadrant + 4, half, f, :].bitcast(I32),
+                    in_=scales_by_pixel[source : source + 4, :].bitcast(I32),
+                )
+
+        raws = [raw_pool.tile([P, HALF_GROUPS, PIXELS], I32, name="raw") for half in range(HALVES)]
+
+        def load_words(half, part):
+            groups = slice(HALF_GROUPS // 2 * part, HALF_GROUPS // 2 * (part + 1))
+            first = HALF_GROUPS * half
+            nc.sync.dma_start(
+                out=raws[half][:, groups, :],
+                in_=filters_words[first + groups.start : first + groups.stop]
+                .rearrange("g p n t -> p g (n t)")
+                .bitcast(I32),
             )
 
         def fill_tile(h, i):
@@ -122,86 +132,83 @@ def tile_localconv2dlayer_e_kernel(tc, x, filters_words, filters_scales, bias, o
         biases = {}
         results = {}
         plan = []
-        done = [0] * CHUNKS
-        while sum(done) < CHUNKS * SIDE_OUT:
+        done = [0] * HALVES
+        while sum(done) < HALVES * SIDE_OUT:
             tick = len(plan)
-            ready = [
-                chunk
-                for chunk in range(CHUNKS)
-                if tick >= FIRST_TICK[chunk] and done[chunk] < min(tick // ROW_TILES - (tick % ROW_TILES == 0), SIDE_OUT)
-            ]
-            plan.append((ready[0], done[ready[0]]) if ready else None)
-            if ready:
+            quantised = min((tick - 1) // ROW_TILES, SIDE_OUT)
+            ready = [half for half in range(HALVES) if tick >= FIRST_TICK[half] and done[half] < quantised]
+            if ready and (tick % 2 == 1 or tick >= TICKS):
+                plan.append((ready[0], done[ready[0]]))
                 done[ready[0]] += 1
+            else:
+                plan.append(None)
         units = [unit for unit in plan if unit is not None]
         movings = {}
         sums_of = {}
 
-        def open_chunk(chunk, bias_from, result_from):
-            bias_sb = bias_from.tile([P, O_CHUNK, PIXELS], BF16, name="bias_sb")
+        def open_half(half, pool):
+            bias_sb = pool.tile([P, O_HALF, PIXELS], BF16, name="bias_sb")
             nc.sync.dma_start(
                 out=bias_sb[:].rearrange("p o n -> p (o n)"),
-                in_=bias[O_CHUNK * chunk : O_CHUNK * (chunk + 1), :].rearrange("o n -> (o n)").partition_broadcast(P),
+                in_=bias[O_HALF * half : O_HALF * (half + 1), :].rearrange("o n -> (o n)").partition_broadcast(P),
             )
-            biases[chunk] = bias_sb
-            result = result_from.tile([P, O_CHUNK, PIXELS], F32, name="result")
-            results[chunk] = result
+            biases[half] = bias_sb
+            result = pool.tile([P, O_HALF, PIXELS], F32, name="result")
+            results[half] = result
 
         def regroup_filters(k):
-            chunk, h = units[k]
-            moving = moving_pool.tile([P, GROUPS_ROW, PASSES, N_MOVING], I32, name="moving", align_bytes=64)
+            half, h = units[k]
+            moving = moving_pool.tile([P, PASSES, SIDE_OUT * O_HALF], I32, name="moving", align_bytes=64)
             nc.vector.tensor_copy(
-                out=moving[:].rearrange("p g f (o q) -> p g f o q", q=PX_GROUP),
-                in_=raws[chunk][:]
-                .rearrange("p (o f) n -> p o f n", f=PASSES)[:, :, :, SIDE_OUT * h : SIDE_OUT * (h + 1)]
-                .rearrange("p o f (g q) -> p g f o q", q=PX_GROUP),
+                out=moving[:].rearrange("p f (n o) -> p f n o", o=O_HALF),
+                in_=raws[half][:].rearrange("p (o f) n -> p f n o", f=PASSES)[
+                    :, :, SIDE_OUT * h : SIDE_OUT * (h + 1), :
+                ],
             )
             movings[k] = moving
 
         def multiply(k):
-            chunk, h = units[k]
+            half, h = units[k]
             moving = movings[k]
-            sums = acc_pool.tile([P, GROUPS_ROW * BANK], F32, name="sums")
-            for g in range(GROUPS_ROW):
-                for q in range(PX_GROUP):
-                    block = IMAGES * (2 * q + g)
-                    in_call = IMAGES * (2 * (q % 2) + g)
-                    for f in range(PASSES):
-                        nc.tensor.matmul_mx(
-                            out=sums[:, BANK * g + N_MOVING * q : BANK * g + N_MOVING * (q + 1)],
-                            lhsT=codes[:, h, f, block : block + IMAGES].bitcast(FP8X4),
-                            lhsT_scale=code_scales[4 * (2 * f + q // 2) : P, h, in_call : in_call + IMAGES],
-                            rhs=moving[:, g, f, :].bitcast(FP8X4),
-                            rhs_scale=filter_scales[:, chunk, GROUPS_ROW * h + g, f, :],
-                            start=(f == 0),
-                            stop=(f == PASSES - 1),
-                        )
+            sums = acc_pool.tile([P, ROW_SUM_BANKS * BANK], F32, name="sums")
+            for w in range(SIDE_OUT):
+                b, e, s = w // 4, w // 2 % 2, w % 2
+                in_call = IMAGES * (2 * s + b)
+                block = TAPS * IMAGES * e + in_call
+                pair = w // PAIR
+                for f in range(PASSES):
+                    scale_columns = slice(
+                        O_HALF * (SIDE_OUT * h + PAIR * pair), O_HALF * (SIDE_OUT * h + PAIR * (pair + 1))
+                    )
+                    nc.tensor.matmul_mx(
+                        out=sums[:, N_MOVING * w : N_MOVING * (w + 1)],
+                        lhsT=codes[:, h, f, block : block + IMAGES].bitcast(FP8X4),
+                        lhsT_scale=code_scales[4 * (2 * f + e) : P, h, in_call : in_call + IMAGES],
+                        rhs=moving[:, f, N_MOVING * pair : N_MOVING * (pair + 1)].bitcast(FP8X4),
+                        rhs_scale=filter_scales[:, half, f, scale_columns],
+                        start=(f == 0),
+                        stop=(f == PASSES - 1),
+                    )
             sums_of[k] = sums
 
         def add_bias(k):
-            chunk, h = units[k]
+            half, h = units[k]
             sums = sums_of[k]
-            step = N_MOVING + 1
-            for g in range(GROUPS_ROW):
-                if g == 0:
-                    own = sums[:, 0 : PX_GROUP * step].rearrange("p (q r) -> p q r", r=step)[
-                        :, :, 0 : N_MOVING - 3 : PX_GROUP
-                    ]
-                else:
-                    own = sums[:, 2 * BANK - PX_GROUP * step : 2 * BANK].rearrange("p (q r) -> p q r", r=step)[
-                        :, :, PX_GROUP:step:PX_GROUP
-                    ]
-                pixels = slice(SIDE_OUT * h + PX_GROUP * g, SIDE_OUT * h + PX_GROUP * (g + 1))
+            for g in range(ROW_SUM_BANKS):
+                own = sums[:, BANK * g : BANK * (g + 1)].rearrange("p (a k o) -> p o a k", k=2 * PAIR, o=O_HALF)[
+                    :, :, :, 0 : 2 * PAIR : 3
+                ]
+                pixels = slice(SIDE_OUT * h + BANK_PX * g, SIDE_OUT * h + BANK_PX * (g + 1))
                 nc.vector.tensor_tensor(
-                    out=results[chunk][:, :, pixels],
-                    in0=own.rearrange("p q o -> p o q"),
-                    in1=biases[chunk][:, :, pixels],
+                    out=results[half][:, :, pixels].rearrange("p o (a b) -> p o a b", b=PAIR),
+                    in0=own,
+                    in1=biases[half][:, :, pixels].rearrange("p o (a b) -> p o a b", b=PAIR),
                     op=mybir.AluOpType.add,
                 )
             if h == SIDE_OUT - 1:
                 nc.scalar.dma_start(
-                    out=out[:, O_CHUNK * chunk : O_CHUNK * (chunk + 1), :, :].rearrange("n o h w -> n o (h w)"),
-                    in_=results[chunk][:],
+                    out=out[:, O_HALF * half : O_HALF * (half + 1), :, :].rearrange("n o h w -> n o (h w)"),
+                    in_=results[half][:],
                 )
 
         def copy_out(h, banks):
@@ -213,14 +220,24 @@ def tile_localconv2dlayer_e_kernel(tc, x, filters_words, filters_scales, bias, o
                 )
 
         filled = {}
+        banks_of = {}
         issued = {"units": 0, "regroups": 0}
 
         def regroup_next():
-            k = issued["regroups"]
-            regroup_filters(k)
-            issued["regroups"] = k + 1
+            regroup_filters(issued["regroups"])
+            issued["regroups"] += 1
 
         def run_tick(tick, transpose_row, pad_row):
+            if tick == SCALE_TICK:
+                reorder_scales()
+                move_scales(0, 0)
+                load_words(0, 1)
+                move_scales(0, 1)
+                move_scales(1, 0, (0, 1))
+                load_words(1, 0)
+                move_scales(1, 0, (2, 3))
+                move_scales(1, 1)
+                load_words(1, 1)
             if tick < TICKS:
                 filled[tick] = fill_tile(tick // ROW_TILES, tick % ROW_TILES)
             if tick - 1 in filled:
@@ -230,16 +247,11 @@ def tile_localconv2dlayer_e_kernel(tc, x, filters_words, filters_scales, bias, o
                 if issued["regroups"] == k:
                     regroup_next()
                 multiply(k)
-                if tick + 1 < len(plan) and plan[tick + 1] is not None:
-                    ahead = plan[tick + 1]
-                    if tick + 1 != FIRST_TICK[ahead[0]]:
-                        regroup_next()
+                if k + 1 < len(units) and units[k + 1] in plan[tick + 1 : tick + 3]:
+                    regroup_next()
                 if k >= 1:
                     add_bias(k - 1)
                 issued["units"] = k + 1
-            for chunk in range(CHUNKS):
-                if tick + 1 == FIRST_TICK[chunk]:
-                    spread_scales(chunk)
             row, i = divmod(tick, ROW_TILES)
             if i == 2 and row + 1 < SIDE_OUT:
                 copy_out(row + 1, banks_of[row + 1])
@@ -247,8 +259,8 @@ def tile_localconv2dlayer_e_kernel(tc, x, filters_words, filters_scales, bias, o
                 pad_row(row + 2)
                 banks_of[row + 2] = transpose_row(row + 2)
 
-        banks_of = {}
         stack.enter_context(tc.manual_schedule())
+        half_pool = stack.enter_context(tc.tile_pool(name="first_half", bufs=1))
         with tc.tile_pool(name="early", bufs=1) as early:
             x_sb = early.tile([P, C_IN, SIDE_IN * SIDE_IN], BF16, name="x_sb")
 
@@ -285,15 +297,15 @@ def tile_localconv2dlayer_e_kernel(tc, x, filters_words, filters_scales, bias, o
 
             for channels in X_HALVES:
                 nc.sync.dma_start(out=x_sb[:, channels, :], in_=x[:, channels, :, :].rearrange("n c h w -> n c (h w)"))
-            for chunk in range(CHUNKS):
-                nc.gpsimd.memset(codes[:, SIDE_OUT - 2 + chunk // PASSES, chunk % PASSES, :].bitcast(F32), 0.0)
             nc.vector.memset(padded[:].bitcast(I32), 0)
             nc.vector.memset(zeros[:].bitcast(I32), 0)
             make_identity(nc, identity[:])
-            for chunk in range(CHUNKS):
-                load_filters(chunk)
-                if chunk < CHUNKS - 1:
-                    open_chunk(chunk, bias_pool, out_pool)
+            nc.gpsimd.memset(filter_scales[:].rearrange("p h f m -> p (h f m)").bitcast(F32), 0.0)
+            nc.gpsimd.memset(scales_loaded[scale_sets:P, :].bitcast(F32), 0.0)
+            for half in range(HALVES):
+                load_scales(half)
+            load_words(0, 0)
+            open_half(0, half_pool)
 
             pad_row(0)
             copy_out(0, transpose_row(0))
@@ -303,7 +315,7 @@ def tile_localconv2dlayer_e_kernel(tc, x, filters_words, filters_scales, bias, o
                 run_tick(tick, transpose_row, pad_row)
 
         with tc.tile_pool(name="late", bufs=1, reuse_waits="tile") as late:
-            open_chunk(CHUNKS - 1, late, late)
+            open_half(1, late)
             for tick in range(X_TICKS, len(plan)):
                 run_tick(tick, transpose_row, pad_row)
             add_bias(len(units) - 1)

@@ -27,6 +27,7 @@ ROW_BANKS = 3
 HALVES = 2
 O_HALF = C_OUT // HALVES
 HALF_GROUPS = PASSES * O_HALF
+O_RUN = 4
 SCALE_ROWS = 16
 PAIR = 2
 ROW_PAIRS = SIDE_OUT // PAIR
@@ -80,8 +81,8 @@ def tile_localconv2dlayer_e_kernel(tc, x, filters_words, filters_scales, bias, o
 
         def reorder_scales():
             nc.vector.tensor_copy(
-                out=scales_by_pixel[:].bitcast(U8).rearrange("z (n o) -> z n o", o=O_HALF),
-                in_=scales_loaded[:].bitcast(U8).rearrange("z (o n) -> z n o", o=O_HALF),
+                out=scales_by_pixel[:].bitcast(U8).rearrange("z (n b i) -> z b n i", n=PIXELS, i=O_RUN),
+                in_=scales_loaded[:].bitcast(U8).rearrange("z (b i n) -> z b n i", n=PIXELS, i=O_RUN),
             )
 
         def move_scales(half, f, quadrants=(0, 1, 2, 3)):
@@ -160,9 +161,9 @@ def tile_localconv2dlayer_e_kernel(tc, x, filters_words, filters_scales, bias, o
             half, h = units[k]
             moving = moving_pool.tile([P, PASSES, SIDE_OUT * O_HALF], I32, name="moving", align_bytes=64)
             nc.vector.tensor_copy(
-                out=moving[:].rearrange("p f (n o) -> p f n o", o=O_HALF),
-                in_=raws[half][:].rearrange("p (o f) n -> p f n o", f=PASSES)[
-                    :, :, SIDE_OUT * h : SIDE_OUT * (h + 1), :
+                out=moving[:].rearrange("p f (n b i) -> p f b n i", n=SIDE_OUT, i=O_RUN),
+                in_=raws[half][:].rearrange("p (b i f) n -> p f b n i", i=O_RUN, f=PASSES)[
+                    :, :, :, SIDE_OUT * h : SIDE_OUT * (h + 1), :
                 ],
             )
             movings[k] = moving

@@ -27,7 +27,8 @@ ROW_BANKS = 3
 HALVES = 2
 O_HALF = C_OUT // HALVES
 HALF_GROUPS = PASSES * O_HALF
-O_RUN = 4
+PIXEL_RUN = 4
+IMAGE_RUN = 4
 SCALE_ROWS = 16
 PAIR = 2
 ROW_PAIRS = SIDE_OUT // PAIR
@@ -81,8 +82,8 @@ def tile_localconv2dlayer_e_kernel(tc, x, filters_words, filters_scales, bias, o
 
         def reorder_scales():
             nc.vector.tensor_copy(
-                out=scales_by_pixel[:].bitcast(U8).rearrange("z (n b i) -> z b n i", n=PIXELS, i=O_RUN),
-                in_=scales_loaded[:].bitcast(U8).rearrange("z (b i n) -> z b n i", n=PIXELS, i=O_RUN),
+                out=scales_by_pixel[:].bitcast(U8).rearrange("z (n i o) -> z n o i", i=PIXEL_RUN, o=O_HALF),
+                in_=scales_loaded[:].bitcast(U8).rearrange("z (o n i) -> z n o i", i=PIXEL_RUN, o=O_HALF),
             )
 
         def move_scales(half, f, quadrants=(0, 1, 2, 3)):
@@ -111,13 +112,13 @@ def tile_localconv2dlayer_e_kernel(tc, x, filters_words, filters_scales, bias, o
             first = ROW * f + 2 * e
             grouped = grouped_pool.tile([P, 2, 2, IMAGES, TAPS], BF16, name="grouped", align_bytes=64)
             nc.scalar.copy(
-                out=grouped[:].bitcast(F32)[:, 0, :, :, :],
-                in_=values[:].bitcast(F32)[:, :, first // 2 : first // 2 + TAPS].rearrange("p n (b u) -> p b n u", u=2),
+                out=grouped[:].bitcast(F32)[:, 0, :, :, :].rearrange("p b n u -> p n b u"),
+                in_=values[:].bitcast(F32)[:, :, first // 2 : first // 2 + TAPS].rearrange("p n (b u) -> p n b u", u=2),
             )
             odd_copy = nc.scalar.copy if h >= ROWS_V and i >= ROW_TILES // 2 else nc.vector.tensor_copy
             odd_copy(
-                out=grouped[:, 1, :, :, :],
-                in_=values[:, :, first + 1 : first + 1 + 2 * TAPS].rearrange("p n (b j) -> p b n j", j=TAPS),
+                out=grouped[:, 1, :, :, :].rearrange("p b n j -> p n b j"),
+                in_=values[:, :, first + 1 : first + 1 + 2 * TAPS].rearrange("p n (b j) -> p n b j", j=TAPS),
             )
             return (f, e, grouped)
 
@@ -161,9 +162,9 @@ def tile_localconv2dlayer_e_kernel(tc, x, filters_words, filters_scales, bias, o
             half, h = units[k]
             moving = moving_pool.tile([P, PASSES, SIDE_OUT * O_HALF], I32, name="moving", align_bytes=64)
             nc.vector.tensor_copy(
-                out=moving[:].rearrange("p f (n b i) -> p f b n i", n=SIDE_OUT, i=O_RUN),
-                in_=raws[half][:].rearrange("p (b i f) n -> p f b n i", i=O_RUN, f=PASSES)[
-                    :, :, :, SIDE_OUT * h : SIDE_OUT * (h + 1), :
+                out=moving[:].rearrange("p f (n i o) -> p f n o i", i=PIXEL_RUN, o=O_HALF),
+                in_=raws[half][:].rearrange("p (o f) (n i) -> p f n o i", f=PASSES, i=PIXEL_RUN)[
+                    :, :, SIDE_OUT // PIXEL_RUN * h : SIDE_OUT // PIXEL_RUN * (h + 1), :, :
                 ],
             )
             movings[k] = moving
@@ -216,8 +217,10 @@ def tile_localconv2dlayer_e_kernel(tc, x, filters_words, filters_scales, bias, o
             words = rows[h % 2][:].bitcast(F32)
             for bank in range(ROW_BANKS):
                 nc.scalar.copy(
-                    out=words[:, :, BANK_PLANES * bank : BANK_PLANES * (bank + 1)],
-                    in_=banks[bank][:].rearrange("p a n -> p n a"),
+                    out=words[:, :, BANK_PLANES * bank : BANK_PLANES * (bank + 1)].rearrange(
+                        "p (m i) a -> p m a i", i=IMAGE_RUN
+                    ),
+                    in_=banks[bank][:].rearrange("p a (m i) -> p m a i", i=IMAGE_RUN),
                 )
 
         filled = {}

@@ -37,7 +37,7 @@ BANK = 512
 BANK_PX = 4
 ROW_SUM_BANKS = SIDE_OUT // BANK_PX
 ROW_TILES = PASSES * TAPS // 2
-ROWS_V = 4
+ROWS_V = 6
 TICKS = SIDE_OUT * ROW_TILES
 X_TICKS = ROW_TILES * (SIDE_OUT - 3)
 SCALE_TICK = 2
@@ -54,7 +54,7 @@ def tile_localconv2dlayer_e_kernel(tc, x, filters_words, filters_scales, bias, o
         keep = stack.enter_context(tc.tile_pool(name="keep", bufs=1))
         raw_pool = stack.enter_context(tc.tile_pool(name="raw_filters", bufs=HALVES))
         moving_pool = stack.enter_context(tc.tile_pool(name="moving", bufs=2))
-        grouped_pool = stack.enter_context(tc.tile_pool(name="grouped", bufs=3))
+        grouped_pool = stack.enter_context(tc.tile_pool(name="grouped", bufs=4))
         bank_pool = stack.enter_context(tc.psum_pool(name="transposed", bufs=4))
         acc_pool = stack.enter_context(tc.psum_pool(name="sums", bufs=2))
 

@@ -38,10 +38,12 @@ BANK_PX = 4
 ROW_SUM_BANKS = SIDE_OUT // BANK_PX
 ROW_TILES = PASSES * TAPS // 2
 ROWS_V = 6
+ROWS_E = 4
 TICKS = SIDE_OUT * ROW_TILES
 X_TICKS = ROW_TILES * (SIDE_OUT - 3)
-SCALE_TICK = 2
+SCALE_TICK = 0
 FIRST_TICK = (16, 24)
+DENSE_TICK = 32
 
 X_HALVES = (slice(0, C_IN // PASSES), slice(C_IN // PASSES, C_IN))
 
@@ -111,7 +113,8 @@ def tile_localconv2dlayer_e_kernel(tc, x, filters_words, filters_scales, bias, o
             values = rows[h % 2]
             first = ROW * f + 2 * e
             grouped = grouped_pool.tile([P, 2, 2, IMAGES, TAPS], BF16, name="grouped", align_bytes=64)
-            nc.scalar.copy(
+            even_copy = nc.vector.tensor_copy if h < ROWS_E and i < ROW_TILES // 2 else nc.scalar.copy
+            even_copy(
                 out=grouped[:].bitcast(F32)[:, 0, :, :, :].rearrange("p b n u -> p n b u"),
                 in_=values[:].bitcast(F32)[:, :, first // 2 : first // 2 + TAPS].rearrange("p n (b u) -> p n b u", u=2),
             )
@@ -139,7 +142,7 @@ def tile_localconv2dlayer_e_kernel(tc, x, filters_words, filters_scales, bias, o
             tick = len(plan)
             quantised = min((tick - 1) // ROW_TILES, SIDE_OUT)
             ready = [half for half in range(HALVES) if tick >= FIRST_TICK[half] and done[half] < quantised]
-            if ready and (tick % 2 == 1 or tick >= TICKS):
+            if ready and (tick % 2 == 1 or tick >= DENSE_TICK):
                 plan.append((ready[0], done[ready[0]]))
                 done[ready[0]] += 1
             else:
@@ -196,22 +199,26 @@ def tile_localconv2dlayer_e_kernel(tc, x, filters_words, filters_scales, bias, o
         def add_bias(k):
             half, h = units[k]
             sums = sums_of[k]
-            for g in range(ROW_SUM_BANKS):
+            parts = 2 if k == len(units) - 1 else 1
+            for part, g in [(part, g) for part in range(parts) for g in range(ROW_SUM_BANKS)]:
+                channels = slice(O_HALF // parts * part, O_HALF // parts * (part + 1))
                 own = sums[:, BANK * g : BANK * (g + 1)].rearrange("p (a k o) -> p o a k", k=2 * PAIR, o=O_HALF)[
-                    :, :, :, 0 : 2 * PAIR : 3
+                    :, channels, :, 0 : 2 * PAIR : 3
                 ]
                 pixels = slice(SIDE_OUT * h + BANK_PX * g, SIDE_OUT * h + BANK_PX * (g + 1))
                 nc.vector.tensor_tensor(
-                    out=results[half][:, :, pixels].rearrange("p o (a b) -> p o a b", b=PAIR),
+                    out=results[half][:, channels, pixels].rearrange("p o (a b) -> p o a b", b=PAIR),
                     in0=own,
-                    in1=biases[half][:, :, pixels].rearrange("p o (a b) -> p o a b", b=PAIR),
+                    in1=biases[half][:, channels, pixels].rearrange("p o (a b) -> p o a b", b=PAIR),
                     op=mybir.AluOpType.add,
                 )
-            if h == SIDE_OUT - 1:
-                nc.scalar.dma_start(
-                    out=out[:, O_HALF * half : O_HALF * (half + 1), :, :].rearrange("n o h w -> n o (h w)"),
-                    in_=results[half][:],
-                )
+                if h == SIDE_OUT - 1 and g == ROW_SUM_BANKS - 1:
+                    nc.scalar.dma_start(
+                        out=out[
+                            :, O_HALF * half + channels.start : O_HALF * half + channels.stop, :, :
+                        ].rearrange("n o h w -> n o (h w)"),
+                        in_=results[half][:, channels, :],
+                    )
 
         def copy_out(h, banks):
             words = rows[h % 2][:].bitcast(F32)

from contextlib import ExitStack

import concourse.mybir as mybir
from concourse.masks import make_identity

BF16 = mybir.dt.bfloat16
F32 = mybir.dt.float32
I32 = mybir.dt.int32
U32 = mybir.dt.uint32
U8 = mybir.dt.uint8
FP8X4 = mybir.dt.float8_e4m3fn_x4

P = 128
IMAGES = 128
C_IN = 64
SIDE_IN = 9
SIDE_OUT = 8
TAPS = 4
C_OUT = 128
PIXELS = SIDE_OUT * SIDE_OUT
PASSES = 2
ROW = SIDE_IN + 1
ROW_WORDS = ROW // 2
ROLL = 8
BANK_PLANES = 4
ROW_BANKS = 3
HALVES = 2
O_HALF = C_OUT // HALVES
HALF_GROUPS = PASSES * O_HALF
PIXEL_RUN = 4
IMAGE_RUN = 4
SCALE_ROWS = 16
PAIR = 2
ROW_PAIRS = SIDE_OUT // PAIR
N_MOVING = PAIR * O_HALF
BANK = 512
BANK_PX = 4
ROW_SUM_BANKS = SIDE_OUT // BANK_PX
ROW_TILES = PASSES * TAPS // 2
ROWS_V = 6
ROWS_E = 4
TICKS = SIDE_OUT * ROW_TILES
X_TICKS = ROW_TILES * (SIDE_OUT - 3)
SCALE_TICK = 0
FIRST_TICK = (16, 24)
DENSE_TICK = 32

X_HALVES = (slice(0, C_IN // PASSES), slice(C_IN // PASSES, C_IN))

FLOPS = 2 * IMAGES * C_IN * TAPS * TAPS * C_OUT * PIXELS


def tile_localconv2dlayer_e_kernel(tc, x, filters_words, filters_scales, bias, out):
    nc = tc.nc
    with ExitStack() as stack:
        keep = stack.enter_context(tc.tile_pool(name="keep", bufs=1))
        raw_pool = stack.enter_context(tc.tile_pool(name="raw_filters", bufs=HALVES))
        moving_pool = stack.enter_context(tc.tile_pool(name="moving", bufs=2))
        grouped_pool = stack.enter_context(tc.tile_pool(name="grouped", bufs=4))
        bank_pool = stack.enter_context(tc.psum_pool(name="transposed", bufs=4))
        acc_pool = stack.enter_context(tc.psum_pool(name="sums", bufs=2))

        identity = keep.tile([P, P], F32, name="identity")
        zeros = keep.tile([P, 2 * P], BF16, name="zeros")
        rows = [keep.tile([P, IMAGES, 2 * ROW_BANKS * BANK_PLANES], BF16, name="row%d" % b) for b in range(2)]
        padded = keep.tile([P, TAPS * C_IN + ROLL, ROW], BF16, name="padded")
        codes = keep.tile([P, SIDE_OUT, PASSES, SIDE_OUT * IMAGES], U32, name="codes", align_bytes=64)
        code_scales = keep.tile([P, SIDE_OUT, TAPS * IMAGES], U8, name="code_scales", align_bytes=64)
        filter_scales = keep.tile([P, HALVES, PASSES, PIXELS * O_HALF], U8, name="filter_scales", align_bytes=64)

        scale_sets = HALVES * PASSES * SCALE_ROWS
        scales_loaded = codes[:, SIDE_OUT - 1, 0, :]
        scales_by_pixel = codes[:, SIDE_OUT - 1, 1, :]

        def load_scales(half):
            sets = slice(PASSES * SCALE_ROWS * half, PASSES * SCALE_ROWS * (half + 1))
            nc.sync.dma_start(
                out=scales_loaded[sets, :].bitcast(I32).rearrange("z (o w) -> z o w", o=O_HALF),
                in_=filters_scales[HALF_GROUPS * half : HALF_GROUPS * (half + 1)]
                .rearrange("g r n -> (g r) n")
                .rearrange("(o z) n -> z o n", z=PASSES * SCALE_ROWS)
                .bitcast(I32),
            )

        def reorder_scales():
            nc.vector.tensor_copy(
                out=scales_by_pixel[:].bitcast(U8).rearrange("z (n i o) -> z n o i", i=PIXEL_RUN, o=O_HALF),
                in_=scales_loaded[:].bitcast(U8).rearrange("z (o n i) -> z n o i", i=PIXEL_RUN, o=O_HALF),
            )

        def move_scales(half, f, quadrants=(0, 1, 2, 3)):
            for quadrant in quadrants:
                source = SCALE_ROWS * (PASSES * half + f) + 4 * quadrant
                nc.sync.dma_start(
                    out=filter_scales[32 * quadrant : 32 * quadrant + 4, half, f, :].bitcast(I32),
                    in_=scales_by_pixel[source : source + 4, :].bitcast(I32),
                )

        raws = [raw_pool.tile([P, HALF_GROUPS, PIXELS], I32, name="raw") for half in range(HALVES)]

        def load_words(half, part):
            groups = slice(HALF_GROUPS // 2 * part, HALF_GROUPS // 2 * (part + 1))
            first = HALF_GROUPS * half
            nc.sync.dma_start(
                out=raws[half][:, groups, :],
                in_=filters_words[first + groups.start : first + groups.stop]
                .rearrange("g p n t -> p g (n t)")
                .bitcast(I32),
            )

        def fill_tile(h, i):
            f, e = divmod(i, TAPS // 2)
            values = rows[h % 2]
            first = ROW * f + 2 * e
            grouped = grouped_pool.tile([P, 2, 2, IMAGES, TAPS], BF16, name="grouped", align_bytes=64)
            even_copy = nc.vector.tensor_copy if h < ROWS_E and i < ROW_TILES // 2 else nc.scalar.copy
            even_copy(
                out=grouped[:].bitcast(F32)[:, 0, :, :, :].rearrange("p b n u -> p n b u"),
                in_=values[:].bitcast(F32)[:, :, first // 2 : first // 2 + TAPS].rearrange("p n (b u) -> p n b u", u=2),
            )
            odd_copy = nc.scalar.copy if h >= ROWS_V and i >= ROW_TILES // 2 else nc.vector.tensor_copy
            odd_copy(
                out=grouped[:, 1, :, :, :].rearrange("p b n j -> p n b j"),
                in_=values[:, :, first + 1 : first + 1 + 2 * TAPS].rearrange("p n (b j) -> p n b j", j=TAPS),
            )
            return (f, e, grouped)

        def quantise(h, item):
            f, e, grouped = item
            columns = slice(TAPS * IMAGES * e, TAPS * IMAGES * (e + 1))
            nc.vector.quantize_mx(
                out=codes[:, h, f, columns].bitcast(FP8X4),
                scales=code_scales[4 * (2 * f + e) : P, h, :],
                in_=grouped[:].rearrange("p s b n j -> p (s b n j)"),
            )

        biases = {}
        results = {}
        plan = []
        done = [0] * HALVES
        while sum(done) < HALVES * SIDE_OUT:
            tick = len(plan)
            quantised = min((tick - 1) // ROW_TILES, SIDE_OUT)
            ready = [half for half in range(HALVES) if tick >= FIRST_TICK[half] and done[half] < quantised]
            if ready and (tick % 2 == 1 or tick >= DENSE_TICK):
                plan.append((ready[0], done[ready[0]]))
                done[ready[0]] += 1
            else:
                plan.append(None)
        units = [unit for unit in plan if unit is not None]
        movings = {}
        sums_of = {}

        def open_half(half, pool):
            bias_sb = pool.tile([P, O_HALF, PIXELS], BF16, name="bias_sb")
            nc.sync.dma_start(
                out=bias_sb[:].rearrange("p o n -> p (o n)"),
                in_=bias[O_HALF * half : O_HALF * (half + 1), :].rearrange("o n -> (o n)").partition_broadcast(P),
            )
            biases[half] = bias_sb
            result = pool.tile([P, O_HALF, PIXELS], F32, name="result")
            results[half] = result

        def regroup_filters(k):
            half, h = units[k]
            moving = moving_pool.tile([P, PASSES, SIDE_OUT * O_HALF], I32, name="moving", align_bytes=64)
            nc.vector.tensor_copy(
                out=moving[:].rearrange("p f (n i o) -> p f n o i", i=PIXEL_RUN, o=O_HALF),
                in_=raws[half][:].rearrange("p (o f) (n i) -> p f n o i", f=PASSES, i=PIXEL_RUN)[
                    :, :, SIDE_OUT // PIXEL_RUN * h : SIDE_OUT // PIXEL_RUN * (h + 1), :, :
                ],
            )
            movings[k] = moving

        def multiply(k):
            half, h = units[k]
            moving = movings[k]
            sums = acc_pool.tile([P, ROW_SUM_BANKS * BANK], F32, name="sums")
            for w in range(SIDE_OUT):
                b, e, s = w // 4, w // 2 % 2, w % 2
                in_call = IMAGES * (2 * s + b)
                block = TAPS * IMAGES * e + in_call
                pair = w // PAIR
                for f in range(PASSES):
                    scale_columns = slice(
                        O_HALF * (SIDE_OUT * h + PAIR * pair), O_HALF * (SIDE_OUT * h + PAIR * (pair + 1))
                    )
                    nc.tensor.matmul_mx(
                        out=sums[:, N_MOVING * w : N_MOVING * (w + 1)],
                        lhsT=codes[:, h, f, block : block + IMAGES].bitcast(FP8X4),
                        lhsT_scale=code_scales[4 * (2 * f + e) : P, h, in_call : in_call + IMAGES],
                        rhs=moving[:, f, N_MOVING * pair : N_MOVING * (pair + 1)].bitcast(FP8X4),
                        rhs_scale=filter_scales[:, half, f, scale_columns],
                        start=(f == 0),
                        stop=(f == PASSES - 1),
                    )
            sums_of[k] = sums

        def add_bias(k):
            half, h = units[k]
            sums = sums_of[k]
            parts = 2 if k == len(units) - 1 else 1
            for part, g in [(part, g) for part in range(parts) for g in range(ROW_SUM_BANKS)]:
                channels = slice(O_HALF // parts * part, O_HALF // parts * (part + 1))
                own = sums[:, BANK * g : BANK * (g + 1)].rearrange("p (a k o) -> p o a k", k=2 * PAIR, o=O_HALF)[
                    :, channels, :, 0 : 2 * PAIR : 3
                ]
                pixels = slice(SIDE_OUT * h + BANK_PX * g, SIDE_OUT * h + BANK_PX * (g + 1))
                nc.vector.tensor_tensor(
                    out=results[half][:, channels, pixels].rearrange("p o (a b) -> p o a b", b=PAIR),
                    in0=own,
                    in1=biases[half][:, channels, pixels].rearrange("p o (a b) -> p o a b", b=PAIR),
                    op=mybir.AluOpType.add,
                )
                if h == SIDE_OUT - 1 and g == ROW_SUM_BANKS - 1:
                    nc.scalar.dma_start(
                        out=out[
                            :, O_HALF * half + channels.start : O_HALF * half + channels.stop, :, :
                        ].rearrange("n o h w -> n o (h w)"),
                        in_=results[half][:, channels, :],
                    )

        def copy_out(h, banks):
            words = rows[h % 2][:].bitcast(F32)
            for bank in range(ROW_BANKS):
                nc.scalar.copy(
                    out=words[:, :, BANK_PLANES * bank : BANK_PLANES * (bank + 1)].rearrange(
                        "p (m i) a -> p m a i", i=IMAGE_RUN
                    ),
                    in_=banks[bank][:].rearrange("p a (m i) -> p m a i", i=IMAGE_RUN),
                )

        filled = {}
        banks_of = {}
        issued = {"units": 0, "regroups": 0}

        def regroup_next():
            regroup_filters(issued["regroups"])
            issued["regroups"] += 1

        def run_tick(tick, transpose_row, pad_row):
            if tick == SCALE_TICK:
                reorder_scales()
                move_scales(0, 0)
                load_words(0, 1)
                move_scales(0, 1)
                move_scales(1, 0, (0, 1))
                load_words(1, 0)
                move_scales(1, 0, (2, 3))
                move_scales(1, 1)
                load_words(1, 1)
            if tick < TICKS:
                filled[tick] = fill_tile(tick // ROW_TILES, tick % ROW_TILES)
            if tick - 1 in filled:
                quantise((tick - 1) // ROW_TILES, filled[tick - 1])
            if tick < len(plan) and plan[tick] is not None:
                k = issued["units"]
                if issued["regroups"] == k:
                    regroup_next()
                multiply(k)
                if k + 1 < len(units) and units[k + 1] in plan[tick + 1 : tick + 3]:
                    regroup_next()
                if k >= 1:
                    add_bias(k - 1)
                issued["units"] = k + 1
            row, i = divmod(tick, ROW_TILES)
            if i == 2 and row + 1 < SIDE_OUT:
                copy_out(row + 1, banks_of[row + 1])
            if i == 3 and row + 2 < SIDE_OUT:
                pad_row(row + 2)
                banks_of[row + 2] = transpose_row(row + 2)

        stack.enter_context(tc.manual_schedule())
        half_pool = stack.enter_context(tc.tile_pool(name="first_half", bufs=1))
        with tc.tile_pool(name="early", bufs=1) as early:
            x_sb = early.tile([P, C_IN, SIDE_IN * SIDE_IN], BF16, name="x_sb")

            def pad_row(h):
                if h == 0:
                    for channels in X_HALVES:
                        nc.vector.tensor_copy(
                            out=padded[:, TAPS * channels.start : TAPS * channels.stop, :].rearrange(
                                "p (c i) w -> p c i w", i=TAPS
                            )[:, :, 1:TAPS, 1:ROW],
                            in_=x_sb[:, channels, 0 : SIDE_IN * (TAPS - 1)].rearrange("p c (i w) -> p c i w", w=SIDE_IN),
                        )
                    return
                bottom = h + TAPS - 2
                place = padded[:, bottom + 1 : bottom + 1 + TAPS * (C_IN - 1) + 1 : TAPS, 1:ROW]
                if bottom < SIDE_IN:
                    nc.scalar.copy(out=place, in_=x_sb[:, :, SIDE_IN * bottom : SIDE_IN * (bottom + 1)])
                else:
                    nc.scalar.copy(out=place, in_=zeros[:, 0:SIDE_IN].unsqueeze(1).to_broadcast([P, C_IN, SIDE_IN]))

            def transpose_row(h):
                source = padded[:].bitcast(F32)
                banks = []
                for bank in range(ROW_BANKS):
                    planes = bank_pool.tile([P, BANK_PLANES, IMAGES], F32, name="planes")
                    for m in range(BANK_PLANES):
                        f, a = divmod(BANK_PLANES * bank + m, ROW_WORDS)
                        if f < PASSES:
                            nc.tensor.transpose(planes[:, m, :], source[:, h + P * f : h + P * (f + 1), a], identity[:])
                        else:
                            nc.tensor.transpose(planes[:, m, :], zeros[:].bitcast(F32), identity[:])
                    banks.append(planes)
                return banks

            for channels in X_HALVES:
                nc.sync.dma_start(out=x_sb[:, channels, :], in_=x[:, channels, :, :].rearrange("n c h w -> n c (h w)"))
            nc.vector.memset(padded[:].bitcast(I32), 0)
            nc.vector.memset(zeros[:].bitcast(I32), 0)
            make_identity(nc, identity[:])
            nc.gpsimd.memset(filter_scales[:].rearrange("p h f m -> p (h f m)").bitcast(F32), 0.0)
            nc.gpsimd.memset(scales_loaded[scale_sets:P, :].bitcast(F32), 0.0)
            for half in range(HALVES):
                load_scales(half)
            load_words(0, 0)
            open_half(0, half_pool)

            pad_row(0)
            copy_out(0, transpose_row(0))
            pad_row(1)
            banks_of[1] = transpose_row(1)
            for tick in range(X_TICKS):
                run_tick(tick, transpose_row, pad_row)

        with tc.tile_pool(name="late", bufs=1, reuse_waits="tile") as late:
            open_half(1, late)
            for tick in range(X_TICKS, len(plan)):
                run_tick(tick, transpose_row, pad_row)
            add_bias(len(units) - 1)
